import numpy as np
import ml_dtypes


def mxq(x, axis, fmt="e4m3"):
    dtype, down = {"e4m3": (ml_dtypes.float8_e4m3fn, 7), "e5m2": (ml_dtypes.float8_e5m2, 14)}[fmt]
    v = np.moveaxis(np.asarray(x, np.float32).astype(ml_dtypes.bfloat16).astype(np.float64), axis, -1)
    blocks = v.reshape(v.shape[:-1] + (-1, 32))
    amax = np.abs(blocks).max(-1, keepdims=True)
    byte = np.maximum(np.where(amax > 0, np.frexp(amax)[1] - 1 + 127, 0) - down, 1)
    scale = np.exp2(byte - 127.0)
    codes = (blocks / scale).astype(np.float32).astype(dtype).astype(np.float64)
    return np.moveaxis((codes * scale).reshape(v.shape), -1, axis)


WIDE = False


def mx_kscale(k):
    if not WIDE:
        return np.ones(k)
    levels = np.array([20, -20, 10, -10, 0])
    a = np.random.permutation(np.resize(levels, k // 512 * 4)).reshape(k // 512, 4)
    idx = np.arange(k)
    return np.exp2(a[idx // 512, idx % 128 // 32])


BF16 = ml_dtypes.bfloat16


def bf(x):
    return np.asarray(x, np.float32).astype(BF16)


def f64(x):
    return np.asarray(x).astype(np.float64)


B, HEAD, NUM_EXPERTS, HEAD_DIM = 1024, 2, 3, 512
EPS = 1e-5
VAR0 = 3e-4


def sigmoid(v):
    return 1.0 / (1.0 + np.exp(-v))


def pre_activation(x1, x2, x3, W, b):
    n = x1.shape[0]
    xs = np.stack([f64(x1).reshape(n, HEAD, HEAD_DIM),
                   f64(x2).reshape(n, HEAD, HEAD_DIM),
                   f64(x3).reshape(n, HEAD, HEAD_DIM)], axis=2)
    y = xs.transpose(1, 2, 0, 3) @ f64(W).transpose(0, 1, 3, 2)
    y = y.transpose(2, 1, 0, 3) + f64(b).transpose(1, 0, 2)
    return y.reshape(n, NUM_EXPERTS * HEAD * HEAD_DIM)


def setup_inputs():
    s = mx_kscale(B)[:, None]
    p = (HEAD, NUM_EXPERTS, HEAD_DIM)
    x10 = bf(np.random.standard_normal((B, HEAD * HEAD_DIM)))
    x20 = bf(np.random.standard_normal((B, HEAD * HEAD_DIM)))
    x30 = bf(np.random.standard_normal((B, HEAD * HEAD_DIM)))
    W = bf(np.random.standard_normal((HEAD, NUM_EXPERTS, HEAD_DIM, HEAD_DIM)) / np.sqrt(HEAD_DIM))
    b = bf(np.random.standard_normal(p) * 0.3)
    gamma = bf(np.sqrt(VAR0) * (1.0 + 0.1 * np.random.standard_normal(p)))
    beta = bf(np.random.standard_normal(p) * 0.3)
    running_mean = bf(np.random.standard_normal(p) * 0.3)
    running_var = bf(VAR0 * np.random.uniform(0.5, 1.5, p))
    g = bf(np.random.standard_normal((B, NUM_EXPERTS * HEAD * HEAD_DIM))
           * np.exp2(np.random.randint(-12, 1, (B, 1))) / s)
    y = pre_activation(x10, x20, x30, W, b)
    return {"x1": bf(f64(x10) * s), "x2": bf(f64(x20) * s), "x3": bf(f64(x30) * s),
            "W": W, "b": b, "gamma": gamma, "beta": beta,
            "running_mean": running_mean, "running_var": running_var,
            "y": np.asarray(y, np.float32), "grad_out": g}


def reference(x1, x2, x3, W, b, gamma, beta, running_mean, running_var, y, grad_out):
    n = x1.shape[0]
    xs = np.stack([f64(x1).reshape(n, HEAD, HEAD_DIM),
                   f64(x2).reshape(n, HEAD, HEAD_DIM),
                   f64(x3).reshape(n, HEAD, HEAD_DIM)], axis=2)
    yf = f64(y).reshape(n, NUM_EXPERTS, HEAD, HEAD_DIM)
    g = f64(grad_out).reshape(n, NUM_EXPERTS, HEAD, HEAD_DIM)
    c = (f64(gamma) * (1.0 / np.sqrt(f64(running_var) + EPS))).transpose(1, 0, 2)
    sg = sigmoid(1.702 * yf)
    dy = g * c * (sg * (1.0 + 1.702 * yf * (1.0 - sg)))
    dq = mxq(dy, 0, "e5m2")
    xq = mxq(xs, 0, "e4m3")
    return dq.transpose(2, 1, 3, 0) @ xq.transpose(1, 2, 0, 3)

@@ -1,0 +1,199 @@
+from contextlib import ExitStack
+
+import concourse.mybir as mybir
+from concourse.masks import make_identity
+
+F32 = mybir.dt.float32
+BF16 = mybir.dt.bfloat16
+U32 = mybir.dt.uint32
+U8 = mybir.dt.uint8
+E4M3_X4 = mybir.dt.float8_e4m3fn_x4
+E5M2_X4 = mybir.dt.float8_e5m2_x4
+ACT = mybir.ActivationFunctionType
+ALU = mybir.AluOpType
+
+P = 128
+PACK = 4
+K_PASS = P * PACK
+TOKENS = 1024
+PASSES = TOKENS // K_PASS
+HEADS = 2
+EXPERTS = 3
+DIM = 512
+F_TILES = DIM // P
+RUN = 4
+EPS = 1e-5
+SLOPE = 1.702
+
+FLOPS = 2 * HEADS * EXPERTS * DIM * DIM * TOKENS
+BYTES = (
+    EXPERTS * TOKENS * HEADS * DIM * 2
+    + TOKENS * HEADS * EXPERTS * DIM * (4 + 2)
+    + 2 * HEADS * EXPERTS * DIM * 2
+    + HEADS * EXPERTS * DIM * DIM * 4
+)
+
+
+def by_token(rows):
+    return rows.rearrange("(p j) w -> p j w", j=PACK)
+
+
+def token_major(tile_ap):
+    return tile_ap.rearrange("p j (r i) -> p r j i", i=RUN)
+
+
+def column_major(tile_ap):
+    return tile_ap.rearrange("p (r i) j -> p r j i", i=RUN)
+
+
+def tile_mom_v_kernel(
+    tc, x1, x2, x3, W, b, gamma, beta, running_mean, running_var, y, grad_out, out
+):
+    nc = tc.nc
+    xs = (x1, x2, x3)
+
+    with ExitStack() as ctx:
+        const = ctx.enter_context(tc.tile_pool(name="const", bufs=1))
+        y_pool = ctx.enter_context(tc.tile_pool(name="y", bufs=4))
+        gx_pool = ctx.enter_context(tc.tile_pool(name="gx", bufs=3))
+        work = ctx.enter_context(tc.tile_pool(name="work", bufs=3))
+        grouped = ctx.enter_context(tc.tile_pool(name="grouped", bufs=2))
+        quantised = ctx.enter_context(tc.tile_pool(name="quantised", bufs=2))
+        result_pool = ctx.enter_context(tc.tile_pool(name="result", bufs=4))
+        psum_setup = ctx.enter_context(tc.psum_pool(name="psum_setup", bufs=1))
+        psum_coef = ctx.enter_context(tc.psum_pool(name="psum_coef", bufs=3))
+        psum_out = ctx.enter_context(tc.psum_pool(name="psum_out", bufs=4))
+
+        n_rows = HEADS * EXPERTS * F_TILES
+        var_row0 = n_rows
+        stats = const.tile([P, P], BF16)
+        nc.vector.memset(stats[:], 0.0)
+        nc.scalar.dma_start(out=stats[0:n_rows, :], in_=gamma.rearrange("h e (m p) -> (h e m) p", p=P))
+        nc.scalar.dma_start(
+            out=stats[var_row0 : var_row0 + n_rows, :], in_=running_var.rearrange("h e (m p) -> (h e m) p", p=P)
+        )
+        ident_bf16 = const.tile([P, P], BF16)
+        make_identity(nc, ident_bf16[:])
+        ident_f32 = const.tile([P, P], F32)
+        make_identity(nc, ident_f32[:])
+
+        stats_t = psum_setup.tile([P, P], BF16)
+        nc.tensor.transpose(stats_t[:], stats[:], ident_bf16[:])
+        var_eps = const.tile([P, n_rows], F32)
+        nc.vector.tensor_scalar_add(out=var_eps[:], in0=stats_t[:, var_row0 : var_row0 + n_rows], scalar1=EPS)
+        std = const.tile([P, n_rows], F32)
+        nc.scalar.activation(out=std[:], in_=var_eps[:], func=ACT.Sqrt)
+        inv_std = const.tile([P, n_rows], F32)
+        nc.vector.reciprocal(out=inv_std[:], in_=std[:])
+        coef = const.tile([P, n_rows], F32)
+        nc.vector.scalar_tensor_tensor(
+            out=coef[:], in0=stats_t[:, 0:n_rows], scalar=-0.5, in1=inv_std[:], op0=ALU.mult, op1=ALU.mult
+        )
+
+        def spread_coef(h, e):
+            coef_all = psum_coef.tile([P, DIM], F32)
+            for m in range(F_TILES):
+                row = (EXPERTS * h + e) * F_TILES + m
+                nc.tensor.matmul(
+                    out=coef_all[:, m * P : (m + 1) * P],
+                    lhsT=coef[:, row : row + 1].to_broadcast([P, P]),
+                    rhs=ident_f32[:],
+                    start=True,
+                    stop=True,
+                )
+            return coef_all
+
+        def finish_chunk(chunk):
+            h, e, c, dy_grouped, codes = chunk
+            dy_codes, dy_scales, x_codes, x_scales = codes
+            nc.vector.quantize_mx(
+                out=dy_codes[:, h, c, :].bitcast(E5M2_X4),
+                scales=dy_scales[:, h, c, :],
+                in_=dy_grouped[:].rearrange("p w j -> p (w j)"),
+            )
+            if c < PASSES - 1:
+                return
+            for m in range(F_TILES):
+                f_cols = slice(m * P, (m + 1) * P)
+                acc = psum_out.tile([P, DIM], F32)
+                for k in range(PASSES):
+                    nc.tensor.matmul_mx(
+                        out=acc[:],
+                        lhsT=dy_codes[:, h, k, f_cols].bitcast(E5M2_X4),
+                        lhsT_scale=dy_scales[:, h, k, f_cols],
+                        rhs=x_codes[:, h, k, :].bitcast(E4M3_X4),
+                        rhs_scale=x_scales[:, h, k, :],
+                        start=(k == 0),
+                        stop=(k == PASSES - 1),
+                    )
+                result = result_pool.tile([P, DIM], F32)
+                nc.scalar.copy(out=result[:], in_=acc[:])
+                nc.sync.dma_start(out=out[h, e, f_cols, :], in_=result[:])
+
+        previous = None
+        for e in range(EXPERTS):
+            dy_codes = quantised.tile([P, HEADS, PASSES, DIM], U32, align_bytes=64)
+            dy_scales = quantised.tile([P, HEADS, PASSES, DIM], U8, align_bytes=64)
+            x_codes = quantised.tile([P, HEADS, PASSES, DIM], U32, align_bytes=64)
+            x_scales = quantised.tile([P, HEADS, PASSES, DIM], U8, align_bytes=64)
+            codes = (dy_codes, dy_scales, x_codes, x_scales)
+            coef_of_head = [spread_coef(h, e) for h in range(HEADS)]
+
+            for c in range(PASSES):
+                tokens = slice(c * K_PASS, (c + 1) * K_PASS)
+                e_cols = slice(e * HEADS * DIM, (e + 1) * HEADS * DIM)
+                y_of_head = []
+                for h in range(HEADS):
+                    y_tile = y_pool.tile([P, PACK, DIM], F32)
+                    q_cols = slice((HEADS * e + h) * DIM, (HEADS * e + h + 1) * DIM)
+                    nc.sync.dma_start(out=y_tile[:], in_=by_token(y[tokens, q_cols]))
+                    y_of_head.append(y_tile)
+                    if h == 0:
+                        g_tile = gx_pool.tile([P, PACK, HEADS * DIM], BF16)
+                        nc.sync.dma_start(out=g_tile[:], in_=by_token(grad_out[tokens, e_cols]))
+                        x_tile = gx_pool.tile([P, PACK, HEADS * DIM], BF16)
+                        nc.sync.dma_start(out=x_tile[:], in_=by_token(xs[e][tokens, :]))
+
+                for h in range(HEADS):
+                    h_cols = slice(h * DIM, (h + 1) * DIM)
+                    y_tile = y_of_head[h]
+
+                    tanh_part = work.tile([P, PACK, DIM], F32)
+                    nc.scalar.activation(out=tanh_part[:], in_=y_tile[:], func=ACT.Tanh, scale=SLOPE / 2)
+                    silu_part = work.tile([P, PACK, DIM], F32)
+                    nc.scalar.activation(out=silu_part[:], in_=y_tile[:], func=ACT.Silu, scale=-SLOPE)
+                    x_grouped = grouped.tile([P, DIM, PACK], BF16, align_bytes=64)
+                    nc.scalar.copy(out=column_major(x_grouped[:]), in_=token_major(x_tile[:, :, h_cols]))
+
+                    nc.vector.scalar_tensor_tensor(
+                        out=tanh_part[:],
+                        in0=tanh_part[:],
+                        scalar=1.0,
+                        in1=coef_of_head[h][:].unsqueeze(1).to_broadcast([P, PACK, DIM]),
+                        op0=ALU.add,
+                        op1=ALU.mult,
+                    )
+                    if previous is not None:
+                        finish_chunk(previous)
+                    nc.vector.scalar_tensor_tensor(
+                        out=silu_part[:],
+                        in0=silu_part[:],
+                        scalar=1.0,
+                        in1=tanh_part[:],
+                        op0=ALU.subtract,
+                        op1=ALU.mult,
+                    )
+                    nc.vector.quantize_mx(
+                        out=x_codes[:, h, c, :].bitcast(E4M3_X4),
+                        scales=x_scales[:, h, c, :],
+                        in_=x_grouped[:].rearrange("p w j -> p (w j)"),
+                    )
+                    dy_grouped = grouped.tile([P, DIM, PACK], BF16, align_bytes=64)
+                    nc.vector.tensor_tensor(
+                        out=column_major(dy_grouped[:]),
+                        in0=token_major(silu_part[:]),
+                        in1=token_major(g_tile[:, :, h_cols]),
+                        op=ALU.mult,
+                    )
+                    previous = (h, e, c, dy_grouped, codes)
+        finish_chunk(previous)

@@ -52,24 +52,28 @@ def tile_mom_v_kernel(
     nc = tc.nc
     xs = (x1, x2, x3)
 
+    groups = [(e, c) for e in range(EXPERTS) for c in range(PASSES)]
+    chunks = [(e, c, h) for (e, c) in groups for h in range(HEADS)]
+    n_chunks = len(chunks)
+
     with ExitStack() as ctx:
         const = ctx.enter_context(tc.tile_pool(name="const", bufs=1))
-        y_pool = ctx.enter_context(tc.tile_pool(name="y", bufs=4))
+        y_pool = ctx.enter_context(tc.tile_pool(name="y", bufs=2 * HEADS))
         gx_pool = ctx.enter_context(tc.tile_pool(name="gx", bufs=3))
         work = ctx.enter_context(tc.tile_pool(name="work", bufs=3))
-        grouped = ctx.enter_context(tc.tile_pool(name="grouped", bufs=2))
+        grouped = ctx.enter_context(tc.tile_pool(name="grouped", bufs=3))
         quantised = ctx.enter_context(tc.tile_pool(name="quantised", bufs=2))
-        result_pool = ctx.enter_context(tc.tile_pool(name="result", bufs=4))
-        psum_setup = ctx.enter_context(tc.psum_pool(name="psum_setup", bufs=1))
-        psum_coef = ctx.enter_context(tc.psum_pool(name="psum_coef", bufs=3))
-        psum_out = ctx.enter_context(tc.psum_pool(name="psum_out", bufs=4))
+        result_pool = ctx.enter_context(tc.tile_pool(name="result", bufs=2 * F_TILES))
+        psum_coef = ctx.enter_context(tc.psum_pool(name="psum_coef", bufs=2 * HEADS))
+        psum_out = ctx.enter_context(tc.psum_pool(name="psum_out", bufs=F_TILES))
+        ctx.enter_context(tc.manual_schedule())
 
         n_rows = HEADS * EXPERTS * F_TILES
         var_row0 = n_rows
         stats = const.tile([P, P], BF16)
         nc.vector.memset(stats[:], 0.0)
-        nc.scalar.dma_start(out=stats[0:n_rows, :], in_=gamma.rearrange("h e (m p) -> (h e m) p", p=P))
-        nc.scalar.dma_start(
+        nc.sync.dma_start(out=stats[0:n_rows, :], in_=gamma.rearrange("h e (m p) -> (h e m) p", p=P))
+        nc.sync.dma_start(
             out=stats[var_row0 : var_row0 + n_rows, :], in_=running_var.rearrange("h e (m p) -> (h e m) p", p=P)
         )
         ident_bf16 = const.tile([P, P], BF16)
@@ -77,7 +81,31 @@ def tile_mom_v_kernel(
         ident_f32 = const.tile([P, P], F32)
         make_identity(nc, ident_f32[:])
 
-        stats_t = psum_setup.tile([P, P], BF16)
+        y_tiles = {}
+        g_tiles = {}
+        x_tiles = {}
+
+        def load_group(k):
+            e, c = groups[k]
+            tokens = slice(c * K_PASS, (c + 1) * K_PASS)
+            e_cols = slice(e * HEADS * DIM, (e + 1) * HEADS * DIM)
+            for h in range(HEADS):
+                y_tile = y_pool.tile([P, PACK, DIM], F32)
+                q_cols = slice((HEADS * e + h) * DIM, (HEADS * e + h + 1) * DIM)
+                nc.sync.dma_start(out=y_tile[:], in_=by_token(y[tokens, q_cols]))
+                y_tiles[HEADS * k + h] = y_tile
+                if h == 0:
+                    g_tile = gx_pool.tile([P, PACK, HEADS * DIM], BF16)
+                    nc.sync.dma_start(out=g_tile[:], in_=by_token(grad_out[tokens, e_cols]))
+                    g_tiles[k] = g_tile
+                    x_tile = gx_pool.tile([P, PACK, HEADS * DIM], BF16)
+                    nc.sync.dma_start(out=x_tile[:], in_=by_token(xs[e][tokens, :]))
+                    x_tiles[k] = x_tile
+
+        load_group(0)
+        load_group(1)
+
+        stats_t = psum_out.tile([P, P], BF16, tag="acc")
         nc.tensor.transpose(stats_t[:], stats[:], ident_bf16[:])
         var_eps = const.tile([P, n_rows], F32)
         nc.vector.tensor_scalar_add(out=var_eps[:], in0=stats_t[:, var_row0 : var_row0 + n_rows], scalar1=EPS)
@@ -90,26 +118,94 @@ def tile_mom_v_kernel(
             out=coef[:], in0=stats_t[:, 0:n_rows], scalar=-0.5, in1=inv_std[:], op0=ALU.mult, op1=ALU.mult
         )
 
-        def spread_coef(h, e):
-            coef_all = psum_coef.tile([P, DIM], F32)
-            for m in range(F_TILES):
-                row = (EXPERTS * h + e) * F_TILES + m
-                nc.tensor.matmul(
-                    out=coef_all[:, m * P : (m + 1) * P],
-                    lhsT=coef[:, row : row + 1].to_broadcast([P, P]),
-                    rhs=ident_f32[:],
-                    start=True,
-                    stop=True,
-                )
-            return coef_all
+        coef_all = {}
+        codes = {}
 
-        def finish_chunk(chunk):
-            h, e, c, dy_grouped, codes = chunk
-            dy_codes, dy_scales, x_codes, x_scales = codes
+        def start_expert(e):
+            for h in range(HEADS):
+                bank = psum_coef.tile([P, DIM], F32)
+                for m in range(F_TILES):
+                    row = (EXPERTS * h + e) * F_TILES + m
+                    nc.tensor.matmul(
+                        out=bank[:, m * P : (m + 1) * P],
+                        lhsT=coef[:, row : row + 1].to_broadcast([P, P]),
+                        rhs=ident_f32[:],
+                        start=True,
+                        stop=True,
+                    )
+                coef_all[(e, h)] = bank
+            dy_codes = quantised.tile([P, HEADS, PASSES, DIM], U32, align_bytes=64)
+            dy_scales = quantised.tile([P, HEADS, PASSES, DIM], U8, align_bytes=64)
+            x_codes = quantised.tile([P, HEADS, PASSES, DIM], U32, align_bytes=64)
+            x_scales = quantised.tile([P, HEADS, PASSES, DIM], U8, align_bytes=64)
+            codes[e] = (dy_codes, dy_scales, x_codes, x_scales)
+
+        tanh_part = {}
+        silu_part = {}
+        x_grouped = {}
+        dy_grouped = {}
+
+        def scalar_stage(i):
+            e, c, h = chunks[i]
+            if c == 0 and h == 0:
+                start_expert(e)
+            tanh_part[i] = work.tile([P, PACK, DIM], F32, name="tanh_part")
+            nc.scalar.activation(out=tanh_part[i][:], in_=y_tiles[i][:], func=ACT.Tanh, scale=SLOPE / 2)
+            silu_part[i] = work.tile([P, PACK, DIM], F32, name="silu_part")
+            nc.scalar.activation(out=silu_part[i][:], in_=y_tiles[i][:], func=ACT.Silu, scale=-SLOPE)
+            x_grouped[i] = grouped.tile([P, DIM, PACK], BF16, name="x_grouped", align_bytes=64)
+            nc.scalar.copy(
+                out=column_major(x_grouped[i][:]),
+                in_=token_major(x_tiles[i // HEADS][:, :, h * DIM : (h + 1) * DIM]),
+            )
+
+        def first_multiply(i):
+            e, c, h = chunks[i]
+            nc.vector.scalar_tensor_tensor(
+                out=tanh_part[i][:],
+                in0=tanh_part[i][:],
+                scalar=1.0,
+                in1=coef_all[(e, h)][:].unsqueeze(1).to_broadcast([P, PACK, DIM]),
+                op0=ALU.add,
+                op1=ALU.mult,
+            )
+
+        def second_multiply(i):
+            nc.vector.scalar_tensor_tensor(
+                out=silu_part[i][:],
+                in0=silu_part[i][:],
+                scalar=1.0,
+                in1=tanh_part[i][:],
+                op0=ALU.subtract,
+                op1=ALU.mult,
+            )
+
+        def third_multiply(i):
+            e, c, h = chunks[i]
+            dy_grouped[i] = grouped.tile([P, DIM, PACK], BF16, name="dy_grouped", align_bytes=64)
+            nc.vector.tensor_tensor(
+                out=column_major(dy_grouped[i][:]),
+                in0=token_major(silu_part[i][:]),
+                in1=token_major(g_tiles[i // HEADS][:, :, h * DIM : (h + 1) * DIM]),
+                op=ALU.mult,
+            )
+
+        def quantise_x(i):
+            e, c, h = chunks[i]
+            x_codes, x_scales = codes[e][2:4]
+            nc.vector.quantize_mx(
+                out=x_codes[:, h, c, :].bitcast(E4M3_X4),
+                scales=x_scales[:, h, c, :],
+                in_=x_grouped[i][:].rearrange("p w j -> p (w j)"),
+            )
+
+        def finish_chunk(i):
+            e, c, h = chunks[i]
+            dy_codes, dy_scales, x_codes, x_scales = codes[e]
             nc.vector.quantize_mx(
                 out=dy_codes[:, h, c, :].bitcast(E5M2_X4),
                 scales=dy_scales[:, h, c, :],
-                in_=dy_grouped[:].rearrange("p w j -> p (w j)"),
+                in_=dy_grouped[i][:].rearrange("p w j -> p (w j)"),
             )
             if c < PASSES - 1:
                 return
@@ -130,70 +226,21 @@ def tile_mom_v_kernel(
                 nc.scalar.copy(out=result[:], in_=acc[:])
                 nc.sync.dma_start(out=out[h, e, f_cols, :], in_=result[:])
 
-        previous = None
-        for e in range(EXPERTS):
-            dy_codes = quantised.tile([P, HEADS, PASSES, DIM], U32, align_bytes=64)
-            dy_scales = quantised.tile([P, HEADS, PASSES, DIM], U8, align_bytes=64)
-            x_codes = quantised.tile([P, HEADS, PASSES, DIM], U32, align_bytes=64)
-            x_scales = quantised.tile([P, HEADS, PASSES, DIM], U8, align_bytes=64)
-            codes = (dy_codes, dy_scales, x_codes, x_scales)
-            coef_of_head = [spread_coef(h, e) for h in range(HEADS)]
-
-            for c in range(PASSES):
-                tokens = slice(c * K_PASS, (c + 1) * K_PASS)
-                e_cols = slice(e * HEADS * DIM, (e + 1) * HEADS * DIM)
-                y_of_head = []
-                for h in range(HEADS):
-                    y_tile = y_pool.tile([P, PACK, DIM], F32)
-                    q_cols = slice((HEADS * e + h) * DIM, (HEADS * e + h + 1) * DIM)
-                    nc.sync.dma_start(out=y_tile[:], in_=by_token(y[tokens, q_cols]))
-                    y_of_head.append(y_tile)
-                    if h == 0:
-                        g_tile = gx_pool.tile([P, PACK, HEADS * DIM], BF16)
-                        nc.sync.dma_start(out=g_tile[:], in_=by_token(grad_out[tokens, e_cols]))
-                        x_tile = gx_pool.tile([P, PACK, HEADS * DIM], BF16)
-                        nc.sync.dma_start(out=x_tile[:], in_=by_token(xs[e][tokens, :]))
-
-                for h in range(HEADS):
-                    h_cols = slice(h * DIM, (h + 1) * DIM)
-                    y_tile = y_of_head[h]
-
-                    tanh_part = work.tile([P, PACK, DIM], F32)
-                    nc.scalar.activation(out=tanh_part[:], in_=y_tile[:], func=ACT.Tanh, scale=SLOPE / 2)
-                    silu_part = work.tile([P, PACK, DIM], F32)
-                    nc.scalar.activation(out=silu_part[:], in_=y_tile[:], func=ACT.Silu, scale=-SLOPE)
-                    x_grouped = grouped.tile([P, DIM, PACK], BF16, align_bytes=64)
-                    nc.scalar.copy(out=column_major(x_grouped[:]), in_=token_major(x_tile[:, :, h_cols]))
-
-                    nc.vector.scalar_tensor_tensor(
-                        out=tanh_part[:],
-                        in0=tanh_part[:],
-                        scalar=1.0,
-                        in1=coef_of_head[h][:].unsqueeze(1).to_broadcast([P, PACK, DIM]),
-                        op0=ALU.add,
-                        op1=ALU.mult,
-                    )
-                    if previous is not None:
-                        finish_chunk(previous)
-                    nc.vector.scalar_tensor_tensor(
-                        out=silu_part[:],
-                        in0=silu_part[:],
-                        scalar=1.0,
-                        in1=tanh_part[:],
-                        op0=ALU.subtract,
-                        op1=ALU.mult,
-                    )
-                    nc.vector.quantize_mx(
-                        out=x_codes[:, h, c, :].bitcast(E4M3_X4),
-                        scales=x_scales[:, h, c, :],
-                        in_=x_grouped[:].rearrange("p w j -> p (w j)"),
-                    )
-                    dy_grouped = grouped.tile([P, DIM, PACK], BF16, align_bytes=64)
-                    nc.vector.tensor_tensor(
-                        out=column_major(dy_grouped[:]),
-                        in0=token_major(silu_part[:]),
-                        in1=token_major(g_tile[:, :, h_cols]),
-                        op=ALU.mult,
-                    )
-                    previous = (h, e, c, dy_grouped, codes)
-        finish_chunk(previous)
+        scalar_stage(0)
+        scalar_stage(1)
+        load_group(2)
+        first_multiply(0)
+        for i in range(n_chunks):
+            if i + 2 < n_chunks:
+                scalar_stage(i + 2)
+            second_multiply(i)
+            if i + 1 < n_chunks:
+                first_multiply(i + 1)
+            if i >= 1:
+                finish_chunk(i - 1)
+            quantise_x(i)
+            third_multiply(i)
+            next_group = i // HEADS + 3
+            if i % HEADS == HEADS - 1 and next_group < len(groups):
+                load_group(next_group)
+        finish_chunk(n_chunks - 1)

@@ -55,6 +55,9 @@ def tile_mom_v_kernel(
     groups = [(e, c) for e in range(EXPERTS) for c in range(PASSES)]
     chunks = [(e, c, h) for (e, c) in groups for h in range(HEADS)]
     n_chunks = len(chunks)
+    last = n_chunks - 1
+    whole = [slice(0, DIM)]
+    tiles_of_128 = [slice(m * P, (m + 1) * P) for m in range(F_TILES)]
 
     with ExitStack() as ctx:
         const = ctx.enter_context(tc.tile_pool(name="const", bufs=1))
@@ -76,43 +79,73 @@ def tile_mom_v_kernel(
         nc.sync.dma_start(
             out=stats[var_row0 : var_row0 + n_rows, :], in_=running_var.rearrange("h e (m p) -> (h e m) p", p=P)
         )
+        warm = const.tile([P, 1], F32)
+        nc.vector.memset(warm[:], 0.0)
+        nc.scalar.activation(out=warm[:], in_=warm[:], func=ACT.Tanh)
         ident_bf16 = const.tile([P, P], BF16)
         make_identity(nc, ident_bf16[:])
         ident_f32 = const.tile([P, P], F32)
         make_identity(nc, ident_f32[:])
+        minus_half = const.tile([P, n_rows], F32)
+        nc.gpsimd.memset(minus_half[:], -0.5)
 
         y_tiles = {}
         g_tiles = {}
         x_tiles = {}
 
-        def load_group(k):
+        def load_y(i, pieces):
+            e, c, h = chunks[i]
+            tokens = slice(c * K_PASS, (c + 1) * K_PASS)
+            col0 = (HEADS * e + h) * DIM
+            y_tile = y_pool.tile([P, PACK, DIM], F32)
+            for cols in pieces:
+                nc.sync.dma_start(
+                    out=y_tile[:, :, cols], in_=by_token(y[tokens, col0 + cols.start : col0 + cols.stop])
+                )
+            y_tiles[i] = y_tile
+
+        def new_gx(k):
+            g_tile = gx_pool.tile([P, PACK, HEADS * DIM], BF16)
+            g_tiles[k] = g_tile
+            x_tile = gx_pool.tile([P, PACK, HEADS * DIM], BF16)
+            x_tiles[k] = x_tile
+
+        def load_g(k, cols):
             e, c = groups[k]
             tokens = slice(c * K_PASS, (c + 1) * K_PASS)
-            e_cols = slice(e * HEADS * DIM, (e + 1) * HEADS * DIM)
-            for h in range(HEADS):
-                y_tile = y_pool.tile([P, PACK, DIM], F32)
-                q_cols = slice((HEADS * e + h) * DIM, (HEADS * e + h + 1) * DIM)
-                nc.sync.dma_start(out=y_tile[:], in_=by_token(y[tokens, q_cols]))
-                y_tiles[HEADS * k + h] = y_tile
-                if h == 0:
-                    g_tile = gx_pool.tile([P, PACK, HEADS * DIM], BF16)
-                    nc.sync.dma_start(out=g_tile[:], in_=by_token(grad_out[tokens, e_cols]))
-                    g_tiles[k] = g_tile
-                    x_tile = gx_pool.tile([P, PACK, HEADS * DIM], BF16)
-                    nc.sync.dma_start(out=x_tile[:], in_=by_token(xs[e][tokens, :]))
-                    x_tiles[k] = x_tile
+            col0 = e * HEADS * DIM
+            nc.sync.dma_start(
+                out=g_tiles[k][:, :, cols], in_=by_token(grad_out[tokens, col0 + cols.start : col0 + cols.stop])
+            )
 
-        load_group(0)
+        def load_x(k, cols):
+            e, c = groups[k]
+            tokens = slice(c * K_PASS, (c + 1) * K_PASS)
+            nc.sync.dma_start(out=x_tiles[k][:, :, cols], in_=by_token(xs[e][tokens, cols]))
+
+        both_heads = slice(0, HEADS * DIM)
+
+        def load_group(k):
+            load_y(HEADS * k, whole)
+            new_gx(k)
+            load_g(k, both_heads)
+            load_x(k, both_heads)
+            load_y(HEADS * k + 1, whole)
+
+        load_y(0, tiles_of_128)
+        load_y(1, whole)
+        new_gx(0)
+        for h in range(HEADS):
+            load_g(0, slice(h * DIM, (h + 1) * DIM))
+            load_x(0, slice(h * DIM, (h + 1) * DIM))
         load_group(1)
 
         stats_t = psum_out.tile([P, P], BF16, tag="acc")
         nc.tensor.transpose(stats_t[:], stats[:], ident_bf16[:])
         var_eps = const.tile([P, n_rows], F32)
         nc.vector.tensor_scalar_add(out=var_eps[:], in0=stats_t[:, var_row0 : var_row0 + n_rows], scalar1=EPS)
-        std = const.tile([P, n_rows], F32)
-        nc.scalar.activation(out=std[:], in_=var_eps[:], func=ACT.Sqrt)
         inv_std = const.tile([P, n_rows], F32)
-        nc.vector.reciprocal(out=inv_std[:], in_=std[:])
+        nc.gpsimd.tensor_tensor(out=inv_std[:], in0=var_eps[:], in1=minus_half[:], op=ALU.pow)
         coef = const.tile([P, n_rows], F32)
         nc.vector.scalar_tensor_tensor(
             out=coef[:], in0=stats_t[:, 0:n_rows], scalar=-0.5, in1=inv_std[:], op0=ALU.mult, op1=ALU.mult
@@ -145,48 +178,58 @@ def tile_mom_v_kernel(
         x_grouped = {}
         dy_grouped = {}
 
-        def scalar_stage(i):
+        def functions(i, pieces):
             e, c, h = chunks[i]
             if c == 0 and h == 0:
                 start_expert(e)
             tanh_part[i] = work.tile([P, PACK, DIM], F32, name="tanh_part")
-            nc.scalar.activation(out=tanh_part[i][:], in_=y_tiles[i][:], func=ACT.Tanh, scale=SLOPE / 2)
             silu_part[i] = work.tile([P, PACK, DIM], F32, name="silu_part")
-            nc.scalar.activation(out=silu_part[i][:], in_=y_tiles[i][:], func=ACT.Silu, scale=-SLOPE)
+            for cols in pieces:
+                nc.scalar.activation(
+                    out=tanh_part[i][:, :, cols], in_=y_tiles[i][:, :, cols], func=ACT.Tanh, scale=SLOPE / 2
+                )
+                nc.scalar.activation(
+                    out=silu_part[i][:, :, cols], in_=y_tiles[i][:, :, cols], func=ACT.Silu, scale=-SLOPE
+                )
+
+        def regroup_x(i):
+            e, c, h = chunks[i]
             x_grouped[i] = grouped.tile([P, DIM, PACK], BF16, name="x_grouped", align_bytes=64)
             nc.scalar.copy(
                 out=column_major(x_grouped[i][:]),
                 in_=token_major(x_tiles[i // HEADS][:, :, h * DIM : (h + 1) * DIM]),
             )
 
-        def first_multiply(i):
+        def first_multiply(i, cols):
             e, c, h = chunks[i]
+            width = cols.stop - cols.start
             nc.vector.scalar_tensor_tensor(
-                out=tanh_part[i][:],
-                in0=tanh_part[i][:],
+                out=tanh_part[i][:, :, cols],
+                in0=tanh_part[i][:, :, cols],
                 scalar=1.0,
-                in1=coef_all[(e, h)][:].unsqueeze(1).to_broadcast([P, PACK, DIM]),
+                in1=coef_all[(e, h)][:, cols].unsqueeze(1).to_broadcast([P, PACK, width]),
                 op0=ALU.add,
                 op1=ALU.mult,
             )
 
-        def second_multiply(i):
+        def second_multiply(i, cols):
             nc.vector.scalar_tensor_tensor(
-                out=silu_part[i][:],
-                in0=silu_part[i][:],
+                out=silu_part[i][:, :, cols],
+                in0=silu_part[i][:, :, cols],
                 scalar=1.0,
-                in1=tanh_part[i][:],
+                in1=tanh_part[i][:, :, cols],
                 op0=ALU.subtract,
                 op1=ALU.mult,
             )
 
-        def third_multiply(i):
+        def third_multiply(i, cols):
             e, c, h = chunks[i]
-            dy_grouped[i] = grouped.tile([P, DIM, PACK], BF16, name="dy_grouped", align_bytes=64)
+            if i not in dy_grouped:
+                dy_grouped[i] = grouped.tile([P, DIM, PACK], BF16, name="dy_grouped", align_bytes=64)
             nc.vector.tensor_tensor(
-                out=column_major(dy_grouped[i][:]),
-                in0=token_major(silu_part[i][:]),
-                in1=token_major(g_tiles[i // HEADS][:, :, h * DIM : (h + 1) * DIM]),
+                out=column_major(dy_grouped[i][:, cols, :]),
+                in0=token_major(silu_part[i][:, :, cols]),
+                in1=token_major(g_tiles[i // HEADS][:, :, h * DIM + cols.start : h * DIM + cols.stop]),
                 op=ALU.mult,
             )
 
@@ -199,48 +242,81 @@ def tile_mom_v_kernel(
                 in_=x_grouped[i][:].rearrange("p w j -> p (w j)"),
             )
 
+        def quantise_dy(i, cols):
+            e, c, h = chunks[i]
+            dy_codes, dy_scales = codes[e][0:2]
+            nc.vector.quantize_mx(
+                out=dy_codes[:, h, c, cols].bitcast(E5M2_X4),
+                scales=dy_scales[:, h, c, cols],
+                in_=dy_grouped[i][:, cols, :].rearrange("p w j -> p (w j)"),
+            )
+
+        accs = {}
+
+        def multiply(e, h, m, k):
+            dy_codes, dy_scales, x_codes, x_scales = codes[e]
+            f_cols = tiles_of_128[m]
+            if k == 0:
+                acc = psum_out.tile([P, DIM], F32)
+                accs[(e, h, m)] = acc
+            nc.tensor.matmul_mx(
+                out=accs[(e, h, m)][:],
+                lhsT=dy_codes[:, h, k, f_cols].bitcast(E5M2_X4),
+                lhsT_scale=dy_scales[:, h, k, f_cols],
+                rhs=x_codes[:, h, k, :].bitcast(E4M3_X4),
+                rhs_scale=x_scales[:, h, k, :],
+                start=(k == 0),
+                stop=(k == PASSES - 1),
+            )
+
+        def store(e, h, m):
+            result = result_pool.tile([P, DIM], F32)
+            nc.scalar.copy(out=result[:], in_=accs[(e, h, m)][:])
+            nc.sync.dma_start(out=out[h, e, tiles_of_128[m], :], in_=result[:])
+
         def finish_chunk(i):
             e, c, h = chunks[i]
-            dy_codes, dy_scales, x_codes, x_scales = codes[e]
-            nc.vector.quantize_mx(
-                out=dy_codes[:, h, c, :].bitcast(E5M2_X4),
-                scales=dy_scales[:, h, c, :],
-                in_=dy_grouped[i][:].rearrange("p w j -> p (w j)"),
-            )
+            quantise_dy(i, whole[0])
             if c < PASSES - 1:
                 return
             for m in range(F_TILES):
-                f_cols = slice(m * P, (m + 1) * P)
-                acc = psum_out.tile([P, DIM], F32)
                 for k in range(PASSES):
-                    nc.tensor.matmul_mx(
-                        out=acc[:],
-                        lhsT=dy_codes[:, h, k, f_cols].bitcast(E5M2_X4),
-                        lhsT_scale=dy_scales[:, h, k, f_cols],
-                        rhs=x_codes[:, h, k, :].bitcast(E4M3_X4),
-                        rhs_scale=x_scales[:, h, k, :],
-                        start=(k == 0),
-                        stop=(k == PASSES - 1),
-                    )
-                result = result_pool.tile([P, DIM], F32)
-                nc.scalar.copy(out=result[:], in_=acc[:])
-                nc.sync.dma_start(out=out[h, e, f_cols, :], in_=result[:])
+                    multiply(e, h, m, k)
+                store(e, h, m)
 
-        scalar_stage(0)
-        scalar_stage(1)
-        load_group(2)
-        first_multiply(0)
+        functions(0, tiles_of_128)
+        functions(1, whole)
+        regroup_x(0)
+        for cols in tiles_of_128:
+            first_multiply(0, cols)
+            second_multiply(0, cols)
         for i in range(n_chunks):
             if i + 2 < n_chunks:
-                scalar_stage(i + 2)
-            second_multiply(i)
+                functions(i + 2, whole)
             if i + 1 < n_chunks:
-                first_multiply(i + 1)
+                regroup_x(i + 1)
+            if i == 0:
+                load_group(2)
+            if i > 0:
+                second_multiply(i, whole[0])
+            if i + 1 < n_chunks:
+                first_multiply(i + 1, whole[0])
             if i >= 1:
                 finish_chunk(i - 1)
-            quantise_x(i)
-            third_multiply(i)
+            if i < last:
+                third_multiply(i, whole[0])
+                quantise_x(i)
             next_group = i // HEADS + 3
             if i % HEADS == HEADS - 1 and next_group < len(groups):
                 load_group(next_group)
-        finish_chunk(n_chunks - 1)
+        e, c, h = chunks[last]
+        quantise_x(last)
+        for m in range(F_TILES):
+            multiply(e, h, m, 0)
+        third_multiply(last, tiles_of_128[0])
+        for m in range(F_TILES):
+            if m + 1 < F_TILES:
+                third_multiply(last, tiles_of_128[m + 1])
+            quantise_dy(last, tiles_of_128[m])
+            multiply(e, h, m, 1)
+            store(e, h, m)

@@ -53,7 +53,7 @@ def tile_mom_v_kernel(
     xs = (x1, x2, x3)
 
     groups = [(e, c) for e in range(EXPERTS) for c in range(PASSES)]
-    chunks = [(e, c, h) for (e, c) in groups for h in range(HEADS)]
+    chunks = [(e, c, h) for e in range(EXPERTS) for h in range(HEADS) for c in range(PASSES)]
     n_chunks = len(chunks)
     last = n_chunks - 1
     whole = [slice(0, DIM)]
@@ -79,15 +79,14 @@ def tile_mom_v_kernel(
         nc.sync.dma_start(
             out=stats[var_row0 : var_row0 + n_rows, :], in_=running_var.rearrange("h e (m p) -> (h e m) p", p=P)
         )
-        warm = const.tile([P, 1], F32)
-        nc.vector.memset(warm[:], 0.0)
-        nc.scalar.activation(out=warm[:], in_=warm[:], func=ACT.Tanh)
         ident_bf16 = const.tile([P, P], BF16)
         make_identity(nc, ident_bf16[:])
         ident_f32 = const.tile([P, P], F32)
         make_identity(nc, ident_f32[:])
-        minus_half = const.tile([P, n_rows], F32)
-        nc.gpsimd.memset(minus_half[:], -0.5)
+
+        def group_of(i):
+            e, c, h = chunks[i]
+            return PASSES * e + c
 
         y_tiles = {}
         g_tiles = {}
@@ -125,27 +124,30 @@ def tile_mom_v_kernel(
 
         both_heads = slice(0, HEADS * DIM)
 
-        def load_group(k):
-            load_y(HEADS * k, whole)
+        def load_gx(k):
             new_gx(k)
             load_g(k, both_heads)
             load_x(k, both_heads)
-            load_y(HEADS * k + 1, whole)
 
         load_y(0, tiles_of_128)
         load_y(1, whole)
         new_gx(0)
+        new_gx(1)
         for h in range(HEADS):
-            load_g(0, slice(h * DIM, (h + 1) * DIM))
-            load_x(0, slice(h * DIM, (h + 1) * DIM))
-        load_group(1)
+            for k in range(PASSES):
+                load_g(k, slice(h * DIM, (h + 1) * DIM))
+                load_x(k, slice(h * DIM, (h + 1) * DIM))
+            load_y(2 + h, whole)
+        load_gx(2)
 
         stats_t = psum_out.tile([P, P], BF16, tag="acc")
         nc.tensor.transpose(stats_t[:], stats[:], ident_bf16[:])
         var_eps = const.tile([P, n_rows], F32)
         nc.vector.tensor_scalar_add(out=var_eps[:], in0=stats_t[:, var_row0 : var_row0 + n_rows], scalar1=EPS)
+        std = const.tile([P, n_rows], F32)
+        nc.scalar.activation(out=std[:], in_=var_eps[:], func=ACT.Sqrt)
         inv_std = const.tile([P, n_rows], F32)
-        nc.gpsimd.tensor_tensor(out=inv_std[:], in0=var_eps[:], in1=minus_half[:], op=ALU.pow)
+        nc.vector.reciprocal(out=inv_std[:], in_=std[:])
         coef = const.tile([P, n_rows], F32)
         nc.vector.scalar_tensor_tensor(
             out=coef[:], in0=stats_t[:, 0:n_rows], scalar=-0.5, in1=inv_std[:], op0=ALU.mult, op1=ALU.mult
@@ -197,7 +199,7 @@ def tile_mom_v_kernel(
             x_grouped[i] = grouped.tile([P, DIM, PACK], BF16, name="x_grouped", align_bytes=64)
             nc.scalar.copy(
                 out=column_major(x_grouped[i][:]),
-                in_=token_major(x_tiles[i // HEADS][:, :, h * DIM : (h + 1) * DIM]),
+                in_=token_major(x_tiles[group_of(i)][:, :, h * DIM : (h + 1) * DIM]),
             )
 
         def first_multiply(i, cols):
@@ -229,7 +231,7 @@ def tile_mom_v_kernel(
             nc.vector.tensor_tensor(
                 out=column_major(dy_grouped[i][:, cols, :]),
                 in0=token_major(silu_part[i][:, :, cols]),
-                in1=token_major(g_tiles[i // HEADS][:, :, h * DIM + cols.start : h * DIM + cols.stop]),
+                in1=token_major(g_tiles[group_of(i)][:, :, h * DIM + cols.start : h * DIM + cols.stop]),
                 op=ALU.mult,
             )
 
@@ -295,8 +297,8 @@ def tile_mom_v_kernel(
                 functions(i + 2, whole)
             if i + 1 < n_chunks:
                 regroup_x(i + 1)
-            if i == 0:
-                load_group(2)
+            if i + 4 < n_chunks:
+                load_y(i + 4, whole)
             if i > 0:
                 second_multiply(i, whole[0])
             if i + 1 < n_chunks:
@@ -306,9 +308,9 @@ def tile_mom_v_kernel(
             if i < last:
                 third_multiply(i, whole[0])
                 quantise_x(i)
-            next_group = i // HEADS + 3
-            if i % HEADS == HEADS - 1 and next_group < len(groups):
-                load_group(next_group)
+            next_group = group_of(i) + 3
+            if chunks[i][2] == HEADS - 1 and next_group < len(groups):
+                load_gx(next_group)
         e, c, h = chunks[last]
         quantise_x(last)
         for m in range(F_TILES):

@@ -21,7 +21,7 @@ HEADS = 2
 EXPERTS = 3
 DIM = 512
 F_TILES = DIM // P
-RUN = 4
+RUN = 8
 EPS = 1e-5
 SLOPE = 1.702
 

@@ -72,15 +72,12 @@ def tile_mom_v_kernel(
         ctx.enter_context(tc.manual_schedule())
 
         n_rows = HEADS * EXPERTS * F_TILES
-        var_row0 = n_rows
-        stats = const.tile([P, P], BF16)
-        nc.vector.memset(stats[:], 0.0)
-        nc.sync.dma_start(out=stats[0:n_rows, :], in_=gamma.rearrange("h e (m p) -> (h e m) p", p=P))
-        nc.sync.dma_start(
-            out=stats[var_row0 : var_row0 + n_rows, :], in_=running_var.rearrange("h e (m p) -> (h e m) p", p=P)
-        )
-        ident_bf16 = const.tile([P, P], BF16)
-        make_identity(nc, ident_bf16[:])
+        var_rows = const.tile([n_rows, P], BF16)
+        nc.sync.dma_start(out=var_rows[:], in_=running_var.rearrange("h e (m p) -> (h e m) p", p=P))
+        gamma_rows = const.tile([n_rows, P], BF16)
+        nc.sync.dma_start(out=gamma_rows[:], in_=gamma.rearrange("h e (m p) -> (h e m) p", p=P))
+        coef_rows = const.tile([P, P], F32)
+        nc.vector.memset(coef_rows[:], 0.0)
         ident_f32 = const.tile([P, P], F32)
         make_identity(nc, ident_f32[:])
 
@@ -140,17 +137,12 @@ def tile_mom_v_kernel(
             load_y(2 + h, whole)
         load_gx(2)
 
-        stats_t = psum_out.tile([P, P], BF16, tag="acc")
-        nc.tensor.transpose(stats_t[:], stats[:], ident_bf16[:])
-        var_eps = const.tile([P, n_rows], F32)
-        nc.vector.tensor_scalar_add(out=var_eps[:], in0=stats_t[:, var_row0 : var_row0 + n_rows], scalar1=EPS)
-        std = const.tile([P, n_rows], F32)
-        nc.scalar.activation(out=std[:], in_=var_eps[:], func=ACT.Sqrt)
-        inv_std = const.tile([P, n_rows], F32)
+        std = const.tile([n_rows, P], F32)
+        nc.scalar.activation(out=std[:], in_=var_rows[:], func=ACT.Sqrt, bias=EPS)
+        inv_std = const.tile([n_rows, P], F32)
         nc.vector.reciprocal(out=inv_std[:], in_=std[:])
-        coef = const.tile([P, n_rows], F32)
         nc.vector.scalar_tensor_tensor(
-            out=coef[:], in0=stats_t[:, 0:n_rows], scalar=-0.5, in1=inv_std[:], op0=ALU.mult, op1=ALU.mult
+            out=coef_rows[0:n_rows, :], in0=gamma_rows[:], scalar=-0.5, in1=inv_std[:], op0=ALU.mult, op1=ALU.mult
         )
 
         coef_all = {}
@@ -163,8 +155,8 @@ def tile_mom_v_kernel(
                     row = (EXPERTS * h + e) * F_TILES + m
                     nc.tensor.matmul(
                         out=bank[:, m * P : (m + 1) * P],
-                        lhsT=coef[:, row : row + 1].to_broadcast([P, P]),
-                        rhs=ident_f32[:],
+                        lhsT=ident_f32[:, row : row + 1].to_broadcast([P, P]),
+                        rhs=coef_rows[:],
                         start=True,
                         stop=True,
                     )

@@ -58,6 +58,7 @@ def tile_mom_v_kernel(
     last = n_chunks - 1
     whole = [slice(0, DIM)]
     tiles_of_128 = [slice(m * P, (m + 1) * P) for m in range(F_TILES)]
+    halves = [slice(n * 256, (n + 1) * 256) for n in range(DIM // 256)]
 
     with ExitStack() as ctx:
         const = ctx.enter_context(tc.tile_pool(name="const", bufs=1))
@@ -126,7 +127,7 @@ def tile_mom_v_kernel(
             load_g(k, both_heads)
             load_x(k, both_heads)
 
-        load_y(0, tiles_of_128)
+        load_y(0, halves)
         load_y(1, whole)
         new_gx(0)
         new_gx(1)
@@ -278,10 +279,10 @@ def tile_mom_v_kernel(
                     multiply(e, h, m, k)
                 store(e, h, m)
 
-        functions(0, tiles_of_128)
+        functions(0, halves)
         functions(1, whole)
         regroup_x(0)
-        for cols in tiles_of_128:
+        for cols in halves:
             first_multiply(0, cols)
             second_multiply(0, cols)
         for i in range(n_chunks):

from contextlib import ExitStack

import concourse.mybir as mybir
from concourse.masks import make_identity

F32 = mybir.dt.float32
BF16 = mybir.dt.bfloat16
U32 = mybir.dt.uint32
U8 = mybir.dt.uint8
E4M3_X4 = mybir.dt.float8_e4m3fn_x4
E5M2_X4 = mybir.dt.float8_e5m2_x4
ACT = mybir.ActivationFunctionType
ALU = mybir.AluOpType

P = 128
PACK = 4
K_PASS = P * PACK
TOKENS = 1024
PASSES = TOKENS // K_PASS
HEADS = 2
EXPERTS = 3
DIM = 512
F_TILES = DIM // P
RUN = 8
EPS = 1e-5
SLOPE = 1.702

FLOPS = 2 * HEADS * EXPERTS * DIM * DIM * TOKENS
BYTES = (
    EXPERTS * TOKENS * HEADS * DIM * 2
    + TOKENS * HEADS * EXPERTS * DIM * (4 + 2)
    + 2 * HEADS * EXPERTS * DIM * 2
    + HEADS * EXPERTS * DIM * DIM * 4
)


def by_token(rows):
    return rows.rearrange("(p j) w -> p j w", j=PACK)


def token_major(tile_ap):
    return tile_ap.rearrange("p j (r i) -> p r j i", i=RUN)


def column_major(tile_ap):
    return tile_ap.rearrange("p (r i) j -> p r j i", i=RUN)


def tile_mom_v_kernel(
    tc, x1, x2, x3, W, b, gamma, beta, running_mean, running_var, y, grad_out, out
):
    nc = tc.nc
    xs = (x1, x2, x3)

    groups = [(e, c) for e in range(EXPERTS) for c in range(PASSES)]
    chunks = [(e, c, h) for e in range(EXPERTS) for h in range(HEADS) for c in range(PASSES)]
    n_chunks = len(chunks)
    last = n_chunks - 1
    whole = [slice(0, DIM)]
    tiles_of_128 = [slice(m * P, (m + 1) * P) for m in range(F_TILES)]
    halves = [slice(n * 256, (n + 1) * 256) for n in range(DIM // 256)]

    with ExitStack() as ctx:
        const = ctx.enter_context(tc.tile_pool(name="const", bufs=1))
        y_pool = ctx.enter_context(tc.tile_pool(name="y", bufs=2 * HEADS))
        gx_pool = ctx.enter_context(tc.tile_pool(name="gx", bufs=3))
        work = ctx.enter_context(tc.tile_pool(name="work", bufs=3))
        grouped = ctx.enter_context(tc.tile_pool(name="grouped", bufs=3))
        quantised = ctx.enter_context(tc.tile_pool(name="quantised", bufs=2))
        result_pool = ctx.enter_context(tc.tile_pool(name="result", bufs=2 * F_TILES))
        psum_coef = ctx.enter_context(tc.psum_pool(name="psum_coef", bufs=2 * HEADS))
        psum_out = ctx.enter_context(tc.psum_pool(name="psum_out", bufs=F_TILES))
        ctx.enter_context(tc.manual_schedule())

        n_rows = HEADS * EXPERTS * F_TILES
        var_rows = const.tile([n_rows, P], BF16)
        nc.sync.dma_start(out=var_rows[:], in_=running_var.rearrange("h e (m p) -> (h e m) p", p=P))
        gamma_rows = const.tile([n_rows, P], BF16)
        nc.sync.dma_start(out=gamma_rows[:], in_=gamma.rearrange("h e (m p) -> (h e m) p", p=P))
        coef_rows = const.tile([P, P], F32)
        nc.vector.memset(coef_rows[:], 0.0)
        ident_f32 = const.tile([P, P], F32)
        make_identity(nc, ident_f32[:])

        def group_of(i):
            e, c, h = chunks[i]
            return PASSES * e + c

        y_tiles = {}
        g_tiles = {}
        x_tiles = {}

        def load_y(i, pieces):
            e, c, h = chunks[i]
            tokens = slice(c * K_PASS, (c + 1) * K_PASS)
            col0 = (HEADS * e + h) * DIM
            y_tile = y_pool.tile([P, PACK, DIM], F32)
            for cols in pieces:
                nc.sync.dma_start(
                    out=y_tile[:, :, cols], in_=by_token(y[tokens, col0 + cols.start : col0 + cols.stop])
                )
            y_tiles[i] = y_tile

        def new_gx(k):
            g_tile = gx_pool.tile([P, PACK, HEADS * DIM], BF16)
            g_tiles[k] = g_tile
            x_tile = gx_pool.tile([P, PACK, HEADS * DIM], BF16)
            x_tiles[k] = x_tile

        def load_g(k, cols):
            e, c = groups[k]
            tokens = slice(c * K_PASS, (c + 1) * K_PASS)
            col0 = e * HEADS * DIM
            nc.sync.dma_start(
                out=g_tiles[k][:, :, cols], in_=by_token(grad_out[tokens, col0 + cols.start : col0 + cols.stop])
            )

        def load_x(k, cols):
            e, c = groups[k]
            tokens = slice(c * K_PASS, (c + 1) * K_PASS)
            nc.sync.dma_start(out=x_tiles[k][:, :, cols], in_=by_token(xs[e][tokens, cols]))

        both_heads = slice(0, HEADS * DIM)

        def load_gx(k):
            new_gx(k)
            load_g(k, both_heads)
            load_x(k, both_heads)

        load_y(0, halves)
        load_y(1, whole)
        new_gx(0)
        new_gx(1)
        for h in range(HEADS):
            for k in range(PASSES):
                load_g(k, slice(h * DIM, (h + 1) * DIM))
                load_x(k, slice(h * DIM, (h + 1) * DIM))
            load_y(2 + h, whole)
        load_gx(2)

        std = const.tile([n_rows, P], F32)
        nc.scalar.activation(out=std[:], in_=var_rows[:], func=ACT.Sqrt, bias=EPS)
        inv_std = const.tile([n_rows, P], F32)
        nc.vector.reciprocal(out=inv_std[:], in_=std[:])
        nc.vector.scalar_tensor_tensor(
            out=coef_rows[0:n_rows, :], in0=gamma_rows[:], scalar=-0.5, in1=inv_std[:], op0=ALU.mult, op1=ALU.mult
        )

        coef_all = {}
        codes = {}

        def start_expert(e):
            for h in range(HEADS):
                bank = psum_coef.tile([P, DIM], F32)
                for m in range(F_TILES):
                    row = (EXPERTS * h + e) * F_TILES + m
                    nc.tensor.matmul(
                        out=bank[:, m * P : (m + 1) * P],
                        lhsT=ident_f32[:, row : row + 1].to_broadcast([P, P]),
                        rhs=coef_rows[:],
                        start=True,
                        stop=True,
                    )
                coef_all[(e, h)] = bank
            dy_codes = quantised.tile([P, HEADS, PASSES, DIM], U32, align_bytes=64)
            dy_scales = quantised.tile([P, HEADS, PASSES, DIM], U8, align_bytes=64)
            x_codes = quantised.tile([P, HEADS, PASSES, DIM], U32, align_bytes=64)
            x_scales = quantised.tile([P, HEADS, PASSES, DIM], U8, align_bytes=64)
            codes[e] = (dy_codes, dy_scales, x_codes, x_scales)

        tanh_part = {}
        silu_part = {}
        x_grouped = {}
        dy_grouped = {}

        def functions(i, pieces):
            e, c, h = chunks[i]
            if c == 0 and h == 0:
                start_expert(e)
            tanh_part[i] = work.tile([P, PACK, DIM], F32, name="tanh_part")
            silu_part[i] = work.tile([P, PACK, DIM], F32, name="silu_part")
            for cols in pieces:
                nc.scalar.activation(
                    out=tanh_part[i][:, :, cols], in_=y_tiles[i][:, :, cols], func=ACT.Tanh, scale=SLOPE / 2
                )
                nc.scalar.activation(
                    out=silu_part[i][:, :, cols], in_=y_tiles[i][:, :, cols], func=ACT.Silu, scale=-SLOPE
                )

        def regroup_x(i):
            e, c, h = chunks[i]
            x_grouped[i] = grouped.tile([P, DIM, PACK], BF16, name="x_grouped", align_bytes=64)
            nc.scalar.copy(
                out=column_major(x_grouped[i][:]),
                in_=token_major(x_tiles[group_of(i)][:, :, h * DIM : (h + 1) * DIM]),
            )

        def first_multiply(i, cols):
            e, c, h = chunks[i]
            width = cols.stop - cols.start
            nc.vector.scalar_tensor_tensor(
                out=tanh_part[i][:, :, cols],
                in0=tanh_part[i][:, :, cols],
                scalar=1.0,
                in1=coef_all[(e, h)][:, cols].unsqueeze(1).to_broadcast([P, PACK, width]),
                op0=ALU.add,
                op1=ALU.mult,
            )

        def second_multiply(i, cols):
            nc.vector.scalar_tensor_tensor(
                out=silu_part[i][:, :, cols],
                in0=silu_part[i][:, :, cols],
                scalar=1.0,
                in1=tanh_part[i][:, :, cols],
                op0=ALU.subtract,
                op1=ALU.mult,
            )

        def third_multiply(i, cols):
            e, c, h = chunks[i]
            if i not in dy_grouped:
                dy_grouped[i] = grouped.tile([P, DIM, PACK], BF16, name="dy_grouped", align_bytes=64)
            nc.vector.tensor_tensor(
                out=column_major(dy_grouped[i][:, cols, :]),
                in0=token_major(silu_part[i][:, :, cols]),
                in1=token_major(g_tiles[group_of(i)][:, :, h * DIM + cols.start : h * DIM + cols.stop]),
                op=ALU.mult,
            )

        def quantise_x(i):
            e, c, h = chunks[i]
            x_codes, x_scales = codes[e][2:4]
            nc.vector.quantize_mx(
                out=x_codes[:, h, c, :].bitcast(E4M3_X4),
                scales=x_scales[:, h, c, :],
                in_=x_grouped[i][:].rearrange("p w j -> p (w j)"),
            )

        def quantise_dy(i, cols):
            e, c, h = chunks[i]
            dy_codes, dy_scales = codes[e][0:2]
            nc.vector.quantize_mx(
                out=dy_codes[:, h, c, cols].bitcast(E5M2_X4),
                scales=dy_scales[:, h, c, cols],
                in_=dy_grouped[i][:, cols, :].rearrange("p w j -> p (w j)"),
            )

        accs = {}

        def multiply(e, h, m, k):
            dy_codes, dy_scales, x_codes, x_scales = codes[e]
            f_cols = tiles_of_128[m]
            if k == 0:
                acc = psum_out.tile([P, DIM], F32)
                accs[(e, h, m)] = acc
            nc.tensor.matmul_mx(
                out=accs[(e, h, m)][:],
                lhsT=dy_codes[:, h, k, f_cols].bitcast(E5M2_X4),
                lhsT_scale=dy_scales[:, h, k, f_cols],
                rhs=x_codes[:, h, k, :].bitcast(E4M3_X4),
                rhs_scale=x_scales[:, h, k, :],
                start=(k == 0),
                stop=(k == PASSES - 1),
            )

        def store(e, h, m):
            result = result_pool.tile([P, DIM], F32)
            nc.scalar.copy(out=result[:], in_=accs[(e, h, m)][:])
            nc.sync.dma_start(out=out[h, e, tiles_of_128[m], :], in_=result[:])

        def finish_chunk(i):
            e, c, h = chunks[i]
            quantise_dy(i, whole[0])
            if c < PASSES - 1:
                return
            for m in range(F_TILES):
                for k in range(PASSES):
                    multiply(e, h, m, k)
                store(e, h, m)

        functions(0, halves)
        functions(1, whole)
        regroup_x(0)
        for cols in halves:
            first_multiply(0, cols)
            second_multiply(0, cols)
        for i in range(n_chunks):
            if i + 2 < n_chunks:
                functions(i + 2, whole)
            if i + 1 < n_chunks:
                regroup_x(i + 1)
            if i + 4 < n_chunks:
                load_y(i + 4, whole)
            if i > 0:
                second_multiply(i, whole[0])
            if i + 1 < n_chunks:
                first_multiply(i + 1, whole[0])
            if i >= 1:
                finish_chunk(i - 1)
            if i < last:
                third_multiply(i, whole[0])
                quantise_x(i)
            next_group = group_of(i) + 3
            if chunks[i][2] == HEADS - 1 and next_group < len(groups):
                load_gx(next_group)
        e, c, h = chunks[last]
        quantise_x(last)
        for m in range(F_TILES):
            multiply(e, h, m, 0)
        third_multiply(last, tiles_of_128[0])
        for m in range(F_TILES):
            if m + 1 < F_TILES:
                third_multiply(last, tiles_of_128[m + 1])
            quantise_dy(last, tiles_of_128[m])
            multiply(e, h, m, 1)
            store(e, h, m)
